import numpy as np
import ml_dtypes


def mxq(x, axis, fmt="e4m3"):
    dtype, down = {"e4m3": (ml_dtypes.float8_e4m3fn, 7), "e5m2": (ml_dtypes.float8_e5m2, 14)}[fmt]
    v = np.moveaxis(np.asarray(x, np.float32).astype(ml_dtypes.bfloat16).astype(np.float64), axis, -1)
    blocks = v.reshape(v.shape[:-1] + (-1, 32))
    amax = np.abs(blocks).max(-1, keepdims=True)
    byte = np.maximum(np.where(amax > 0, np.frexp(amax)[1] - 1 + 127, 0) - down, 1)
    scale = np.exp2(byte - 127.0)
    codes = (blocks / scale).astype(np.float32).astype(dtype).astype(np.float64)
    return np.moveaxis((codes * scale).reshape(v.shape), -1, axis)


WIDE = False


def mx_kscale(k):
    if not WIDE:
        return np.ones(k)
    levels = np.array([10, -10, 5, -5, 0])
    if k % 512:
        return np.exp2(np.random.permutation(np.resize(levels, k // 32))).repeat(32)
    a = np.empty((k // 512, 16))
    for p in range(k // 512):
        a[p, :8] = np.random.permutation(np.resize(levels, 8))
        for g in range(8):
            far = levels[np.abs(levels - a[p, g]) >= 10]
            a[p, g + 8] = far[np.random.randint(len(far))]
    return np.exp2(a.ravel()).repeat(32)


BF16 = ml_dtypes.bfloat16


def bf(x):
    return np.asarray(x, np.float32).astype(BF16)


def f64(x):
    return np.asarray(x).astype(np.float64)


NU, NI, D = 1024, 1024, 512
N = NU + NI


def setup_inputs():
    s, t = mx_kscale(N), mx_kscale(D)
    return {"A": bf(np.random.uniform(0.0, 2.0 / np.sqrt(N), (N, N)) * s),
            "features": bf(np.random.standard_normal((N, D)) / s[:, None] * t),
            "Wg": bf(np.random.standard_normal((D, D)) / np.sqrt(D) / t[:, None]),
            "bg": bf(np.random.standard_normal(D) * 0.1)}


def reference(A, features, Wg, bg):
    agg = mxq(f64(A), 1, "e4m3") @ mxq(f64(features), 0, "e4m3")
    return np.maximum((mxq(agg, 1, "e4m3") @ mxq(f64(Wg), 0, "e4m3")) + f64(bg), 0.0)

@@ -1,0 +1,244 @@
+from contextlib import ExitStack
+
+import concourse.mybir as mybir
+from concourse.masks import make_identity
+
+F32 = mybir.dt.float32
+BF16 = mybir.dt.bfloat16
+U32 = mybir.dt.uint32
+U8 = mybir.dt.uint8
+FP8X4 = mybir.dt.float8_e4m3fn_x4
+
+P = 128
+PACK = 4
+K_PASS = P * PACK
+NODES = 2048
+FEAT = 512
+A_PASSES = NODES // K_PASS
+FEAT_BLOCKS = FEAT // P
+NODE_TILES = NODES // P
+TILES_PER_ROUND = 2
+ROUND_NODES = TILES_PER_ROUND * P
+ROUNDS = NODE_TILES // TILES_PER_ROUND
+AHEAD = 2
+PLANES_PER_BANK = 4
+BANKS_PER_TILE = NODES // 2 // P // PLANES_PER_BANK
+XT_BANKS = 4
+AGG_BANKS = 2
+BLOCKS_PER_BANK = FEAT_BLOCKS // AGG_BANKS
+OUT_BANKS = 2
+
+FLOPS = 2 * NODES * NODES * FEAT + 2 * NODES * FEAT * FEAT
+
+
+def tile_net_pa_kernel(tc, A, features, Wg, bg, out):
+    nc = tc.nc
+    with ExitStack() as ctx:
+        keep = ctx.enter_context(tc.tile_pool(name="keep", bufs=1))
+        a_pool = ctx.enter_context(tc.tile_pool(name="a_rows", bufs=NODE_TILES))
+        raw_pool = ctx.enter_context(tc.tile_pool(name="raw", bufs=A_PASSES + 1))
+        regroup_pool = ctx.enter_context(tc.tile_pool(name="regroup", bufs=2))
+        stream = ctx.enter_context(tc.tile_pool(name="stream", bufs=2))
+        result_pool = ctx.enter_context(tc.tile_pool(name="result", bufs=2 * TILES_PER_ROUND))
+        xt_pool = ctx.enter_context(tc.psum_pool(name="xt", bufs=XT_BANKS))
+        agg_pool = ctx.enter_context(tc.psum_pool(name="agg", bufs=AGG_BANKS))
+        out_pool = ctx.enter_context(tc.psum_pool(name="outp", bufs=OUT_BANKS))
+        ctx.enter_context(tc.manual_schedule())
+
+        bias_row = keep.tile([P, FEAT], BF16)
+        nc.vector.memset(bias_row[:], 0.0)
+        nc.scalar.dma_start(out=bias_row[0:1, :], in_=bg.unsqueeze(0))
+
+        f_raw = []
+        for g in range(A_PASSES):
+            raw = raw_pool.tile([P, PACK, FEAT], BF16, name="f_raw%d" % g, tag="raw")
+            nc.sync.dma_start(
+                out=raw[:],
+                in_=features[g * K_PASS : (g + 1) * K_PASS, :].rearrange(
+                    "(p j) c -> p j c", j=PACK
+                ),
+            )
+            f_raw.append(raw)
+
+        a_rows = []
+
+        def load_a(j):
+            rows = a_pool.tile([P, NODES], BF16, name="a_rows%d" % j, tag="a_rows")
+            nc.sync.dma_start(out=rows[:], in_=A[j * P : (j + 1) * P, :])
+            a_rows.append(rows)
+
+        for j in range(AHEAD * TILES_PER_ROUND):
+            load_a(j)
+        w_raw = raw_pool.tile([P, PACK, FEAT], BF16, name="w_raw", tag="raw")
+        nc.sync.dma_start(out=w_raw[:], in_=Wg.rearrange("(p t) n -> p t n", t=PACK))
+        for j in range(AHEAD * TILES_PER_ROUND, NODE_TILES):
+            load_a(j)
+
+        ident = keep.tile([P, P], F32)
+        make_identity(nc, ident[:])
+        ones = keep.tile([P, P], BF16)
+        nc.vector.memset(ones[:], 1.0)
+
+        f_codes = keep.tile([P, A_PASSES, FEAT], U32, align_bytes=64)
+        f_scales = keep.tile([P, A_PASSES, FEAT], U8, align_bytes=64)
+        w_codes = keep.tile([P, FEAT], U32, align_bytes=64)
+        w_scales = keep.tile([P, FEAT], U8, align_bytes=64)
+
+        half = FEAT // 2
+
+        def regroup_features(raw, name):
+            grouped = regroup_pool.tile(
+                [P, FEAT, PACK], BF16, name=name, tag="grouped", align_bytes=64
+            )
+            columns = raw[:].rearrange("p j (m t) -> p t m j", t=FEAT_BLOCKS)
+            blocks = grouped[:].rearrange("p (t m) j -> p t m j", t=FEAT_BLOCKS)
+            first = FEAT_BLOCKS // 2
+            nc.vector.tensor_copy(out=blocks[:, :first], in_=columns[:, :first])
+            nc.scalar.copy(out=blocks[:, first:], in_=columns[:, first:])
+            return grouped
+
+        def regroup_weights(raw, name):
+            grouped = regroup_pool.tile(
+                [P, FEAT, PACK], BF16, name=name, tag="grouped", align_bytes=64
+            )
+            nc.vector.tensor_copy(
+                out=grouped[:, :half, :].rearrange("p (c i) t -> p c t i", i=4),
+                in_=raw[:, :, :half].rearrange("p t (c i) -> p c t i", i=4),
+            )
+            nc.scalar.copy(
+                out=grouped[:, half:, :].rearrange("p (c i) t -> p c t i", i=4),
+                in_=raw[:, :, half:].rearrange("p t (c i) -> p c t i", i=4),
+            )
+            return grouped
+
+        def quantise(grouped, codes, scales):
+            nc.vector.quantize_mx(
+                out=codes.bitcast(FP8X4),
+                scales=scales,
+                in_=grouped[:].rearrange("p c t -> p (c t)"),
+            )
+
+        f_grouped = []
+        for g in range(A_PASSES):
+            f_grouped.append(regroup_features(f_raw[g], "f_grouped%d" % g))
+            if g >= 1:
+                quantise(f_grouped[g - 1], f_codes[:, g - 1, :], f_scales[:, g - 1, :])
+        quantise(f_grouped[A_PASSES - 1], f_codes[:, A_PASSES - 1, :], f_scales[:, A_PASSES - 1, :])
+
+        a_grouped = {}
+        a_codes = {}
+        a_scales = {}
+        agg_codes = {}
+        agg_scales = {}
+        passes_per_bank = PLANES_PER_BANK // 2
+        bank_columns = passes_per_bank * ROUND_NODES
+
+        def transpose_a(i):
+            grouped = stream.tile(
+                [P, A_PASSES * ROUND_NODES * PACK], BF16, name="a_grouped", align_bytes=64
+            )
+            grouped_words = grouped[:].bitcast(F32).rearrange(
+                "p (g s r u) -> p g s r u", g=A_PASSES, s=TILES_PER_ROUND, u=2
+            )
+            for s in range(TILES_PER_ROUND):
+                words = a_rows[i * TILES_PER_ROUND + s][:].bitcast(F32)
+                for h in range(BANKS_PER_TILE):
+                    xt = xt_pool.tile([P, PLANES_PER_BANK, P], F32, name="xt")
+                    for b in range(PLANES_PER_BANK):
+                        g, u = divmod(h * PLANES_PER_BANK + b, 2)
+                        nc.tensor.transpose(
+                            xt[:, b, :], words[:, 2 * P * g + u : 2 * P * (g + 1) : 2], ident[:]
+                        )
+                    nc.scalar.copy(
+                        out=grouped_words[:, h * passes_per_bank : (h + 1) * passes_per_bank, s],
+                        in_=xt[:].rearrange("p (g u) r -> p g r u", u=2),
+                    )
+            a_grouped[i] = grouped
+
+        def quantise_a(i):
+            codes = stream.tile([P, A_PASSES * ROUND_NODES], U32, name="a_codes", align_bytes=64)
+            scales = stream.tile([P, A_PASSES * ROUND_NODES], U8, name="a_scales", align_bytes=64)
+            for h in range(BANKS_PER_TILE):
+                nc.vector.quantize_mx(
+                    out=codes[:, h * bank_columns : (h + 1) * bank_columns].bitcast(FP8X4),
+                    scales=scales[:, h * bank_columns : (h + 1) * bank_columns],
+                    in_=a_grouped[i][:, h * bank_columns * PACK : (h + 1) * bank_columns * PACK],
+                )
+            a_codes[i] = codes
+            a_scales[i] = scales
+
+        def aggregate(i):
+            grouped = stream.tile([P, ROUND_NODES, PACK], BF16, name="agg_grouped", align_bytes=64)
+            for b in range(AGG_BANKS):
+                agg = agg_pool.tile([P, BLOCKS_PER_BANK, ROUND_NODES], F32, name="agg")
+                for t in range(BLOCKS_PER_BANK):
+                    block = (b * BLOCKS_PER_BANK + t) * P
+                    for g in range(A_PASSES):
+                        nc.tensor.matmul_mx(
+                            out=agg[:, t, :],
+                            lhsT=f_codes[:, g, block : block + P].bitcast(FP8X4),
+                            lhsT_scale=f_scales[:, g, block : block + P],
+                            rhs=a_codes[i][:, g * ROUND_NODES : (g + 1) * ROUND_NODES].bitcast(FP8X4),
+                            rhs_scale=a_scales[i][:, g * ROUND_NODES : (g + 1) * ROUND_NODES],
+                            start=(g == 0),
+                            stop=(g == A_PASSES - 1),
+                        )
+                nc.scalar.copy(
+                    out=grouped[:, :, b * BLOCKS_PER_BANK : (b + 1) * BLOCKS_PER_BANK],
+                    in_=agg[:].rearrange("p t n -> p n t"),
+                )
+            codes = stream.tile([P, ROUND_NODES], U32, name="agg_codes", align_bytes=64)
+            scales = stream.tile([P, ROUND_NODES], U8, name="agg_scales", align_bytes=64)
+            quantise(grouped, codes[:], scales[:])
+            agg_codes[i] = codes
+            agg_scales[i] = scales
+
+        result = {}
+
+        def project(j):
+            first = (j % TILES_PER_ROUND) * P
+            nodes = slice(first, first + P)
+            out_psum = out_pool.tile([P, FEAT], F32, name="out_psum")
+            nc.tensor.matmul_mx(
+                out=out_psum[:],
+                lhsT=agg_codes[j // TILES_PER_ROUND][:, nodes].bitcast(FP8X4),
+                lhsT_scale=agg_scales[j // TILES_PER_ROUND][:, nodes],
+                rhs=w_codes[:].bitcast(FP8X4),
+                rhs_scale=w_scales[:],
+                start=True,
+                stop=True,
+            )
+            result[j] = result_pool.tile([P, FEAT], F32, name="result")
+            nc.vector.tensor_tensor(
+                out=result[j][:], in0=out_psum[:], in1=bias[:], op=mybir.AluOpType.add
+            )
+
+        def finish(j):
+            nc.vector.tensor_scalar_max(out=result[j][:], in0=result[j][:], scalar1=0.0)
+            nc.sync.dma_start(out=out[j * P : (j + 1) * P, :], in_=result[j][:])
+
+        def tiles_of(i):
+            return range(i * TILES_PER_ROUND, (i + 1) * TILES_PER_ROUND)
+
+        transpose_a(0)
+        quantise_a(0)
+        for i in range(1, AHEAD):
+            transpose_a(i)
+        bias_psum = out_pool.tile([P, FEAT], F32, name="bias_psum", tag="out_psum")
+        nc.tensor.matmul(out=bias_psum[:], lhsT=ones[:], rhs=bias_row[:], start=True, stop=True)
+        bias = keep.tile([P, FEAT], F32)
+        nc.scalar.copy(out=bias[:], in_=bias_psum[:])
+        quantise(regroup_weights(w_raw, "w_grouped"), w_codes[:], w_scales[:])
+
+        for i in range(ROUNDS + 1):
+            if i + 1 < ROUNDS:
+                quantise_a(i + 1)
+            if i < ROUNDS:
+                aggregate(i)
+            if i >= 1:
+                for j in tiles_of(i - 1):
+                    project(j)
+                for j in tiles_of(i - 1):
+                    finish(j)
+            if i + AHEAD < ROUNDS:
+                transpose_a(i + AHEAD)

@@ -17,16 +17,17 @@ FEAT = 512
 A_PASSES = NODES // K_PASS
 FEAT_BLOCKS = FEAT // P
 NODE_TILES = NODES // P
+HEAD_TILES = 4
+HEAD_NODES = HEAD_TILES * P
 TILES_PER_ROUND = 2
 ROUND_NODES = TILES_PER_ROUND * P
-ROUNDS = NODE_TILES // TILES_PER_ROUND
-AHEAD = 2
+ROUNDS = (NODE_TILES - HEAD_TILES) // TILES_PER_ROUND
 PLANES_PER_BANK = 4
 BANKS_PER_TILE = NODES // 2 // P // PLANES_PER_BANK
 XT_BANKS = 4
 AGG_BANKS = 2
-BLOCKS_PER_BANK = FEAT_BLOCKS // AGG_BANKS
 OUT_BANKS = 2
+BLOCKS_PER_BANK = FEAT_BLOCKS // AGG_BANKS
 
 FLOPS = 2 * NODES * NODES * FEAT + 2 * NODES * FEAT * FEAT
 
@@ -35,22 +36,33 @@ def tile_net_pa_kernel(tc, A, features, Wg, bg, out):
     nc = tc.nc
     with ExitStack() as ctx:
         keep = ctx.enter_context(tc.tile_pool(name="keep", bufs=1))
-        a_pool = ctx.enter_context(tc.tile_pool(name="a_rows", bufs=NODE_TILES))
+        a_pool = ctx.enter_context(
+            tc.tile_pool(name="a_rows", bufs=NODE_TILES - HEAD_TILES)
+        )
         raw_pool = ctx.enter_context(tc.tile_pool(name="raw", bufs=A_PASSES + 1))
+        head_pool = ctx.enter_context(tc.tile_pool(name="head", bufs=A_PASSES))
         regroup_pool = ctx.enter_context(tc.tile_pool(name="regroup", bufs=2))
-        stream = ctx.enter_context(tc.tile_pool(name="stream", bufs=2))
-        result_pool = ctx.enter_context(tc.tile_pool(name="result", bufs=2 * TILES_PER_ROUND))
+        stream = ctx.enter_context(tc.tile_pool(name="stream", bufs=3))
+        result_pool = ctx.enter_context(tc.tile_pool(name="result", bufs=8))
         xt_pool = ctx.enter_context(tc.psum_pool(name="xt", bufs=XT_BANKS))
-        agg_pool = ctx.enter_context(tc.psum_pool(name="agg", bufs=AGG_BANKS))
-        out_pool = ctx.enter_context(tc.psum_pool(name="outp", bufs=OUT_BANKS))
+        bank_pool = ctx.enter_context(tc.psum_pool(name="banks", bufs=1))
         ctx.enter_context(tc.manual_schedule())
 
         bias_row = keep.tile([P, FEAT], BF16)
         nc.vector.memset(bias_row[:], 0.0)
         nc.scalar.dma_start(out=bias_row[0:1, :], in_=bg.unsqueeze(0))
 
+        a_head = []
         f_raw = []
         for g in range(A_PASSES):
+            rows = head_pool.tile([P, HEAD_TILES, K_PASS], BF16, name="a_head%d" % g, tag="a_head")
+            nc.sync.dma_start(
+                out=rows[:],
+                in_=A[0:HEAD_NODES, g * K_PASS : (g + 1) * K_PASS].rearrange(
+                    "(s p) k -> p s k", p=P
+                ),
+            )
+            a_head.append(rows)
             raw = raw_pool.tile([P, PACK, FEAT], BF16, name="f_raw%d" % g, tag="raw")
             nc.sync.dma_start(
                 out=raw[:],
@@ -60,71 +72,104 @@ def tile_net_pa_kernel(tc, A, features, Wg, bg, out):
             )
             f_raw.append(raw)
 
-        a_rows = []
+        a_rows = {}
 
         def load_a(j):
-            rows = a_pool.tile([P, NODES], BF16, name="a_rows%d" % j, tag="a_rows")
-            nc.sync.dma_start(out=rows[:], in_=A[j * P : (j + 1) * P, :])
-            a_rows.append(rows)
+            a_rows[j] = a_pool.tile([P, NODES], BF16, name="a_rows%d" % j, tag="a_rows")
+            nc.sync.dma_start(out=a_rows[j][:], in_=A[j * P : (j + 1) * P, :])
 
-        for j in range(AHEAD * TILES_PER_ROUND):
+        for j in range(HEAD_TILES, HEAD_TILES + TILES_PER_ROUND):
             load_a(j)
         w_raw = raw_pool.tile([P, PACK, FEAT], BF16, name="w_raw", tag="raw")
         nc.sync.dma_start(out=w_raw[:], in_=Wg.rearrange("(p t) n -> p t n", t=PACK))
-        for j in range(AHEAD * TILES_PER_ROUND, NODE_TILES):
+        for j in range(HEAD_TILES + TILES_PER_ROUND, NODE_TILES):
             load_a(j)
 
         ident = keep.tile([P, P], F32)
         make_identity(nc, ident[:])
         ones = keep.tile([P, P], BF16)
         nc.vector.memset(ones[:], 1.0)
+        bias = keep.tile([P, FEAT], F32)
 
         f_codes = keep.tile([P, A_PASSES, FEAT], U32, align_bytes=64)
         f_scales = keep.tile([P, A_PASSES, FEAT], U8, align_bytes=64)
         w_codes = keep.tile([P, FEAT], U32, align_bytes=64)
         w_scales = keep.tile([P, FEAT], U8, align_bytes=64)
 
-        half = FEAT // 2
+        def quantise(grouped, codes, scales):
+            nc.vector.quantize_mx(out=codes.bitcast(FP8X4), scales=scales, in_=grouped)
 
-        def regroup_features(raw, name):
+        V_BLOCKS = 3
+
+        def regroup_features(g):
             grouped = regroup_pool.tile(
-                [P, FEAT, PACK], BF16, name=name, tag="grouped", align_bytes=64
+                [P, FEAT * PACK], BF16, name="f_grouped%d" % g, tag="grouped", align_bytes=64
             )
-            columns = raw[:].rearrange("p j (m t) -> p t m j", t=FEAT_BLOCKS)
-            blocks = grouped[:].rearrange("p (t m) j -> p t m j", t=FEAT_BLOCKS)
-            first = FEAT_BLOCKS // 2
-            nc.vector.tensor_copy(out=blocks[:, :first], in_=columns[:, :first])
-            nc.scalar.copy(out=blocks[:, first:], in_=columns[:, first:])
+            columns = f_raw[g][:].rearrange("p j (m t) -> p t m j", t=FEAT_BLOCKS)
+            blocks = grouped[:].rearrange("p (t m j) -> p t m j", t=FEAT_BLOCKS, j=PACK)
+            nc.vector.tensor_copy(out=blocks[:, :2], in_=columns[:, :2])
+            nc.vector.tensor_copy(out=blocks[:, 2], in_=columns[:, 2])
+            nc.scalar.copy(out=blocks[:, V_BLOCKS], in_=columns[:, V_BLOCKS])
             return grouped
 
-        def regroup_weights(raw, name):
+        def regroup_weights():
             grouped = regroup_pool.tile(
-                [P, FEAT, PACK], BF16, name=name, tag="grouped", align_bytes=64
+                [P, FEAT * PACK], BF16, name="w_grouped", tag="grouped", align_bytes=64
             )
             nc.vector.tensor_copy(
-                out=grouped[:, :half, :].rearrange("p (c i) t -> p c t i", i=4),
-                in_=raw[:, :, :half].rearrange("p t (c i) -> p c t i", i=4),
-            )
-            nc.scalar.copy(
-                out=grouped[:, half:, :].rearrange("p (c i) t -> p c t i", i=4),
-                in_=raw[:, :, half:].rearrange("p t (c i) -> p c t i", i=4),
+                out=grouped[:].rearrange("p (c i t) -> p c t i", i=4, t=PACK),
+                in_=w_raw[:].rearrange("p t (c i) -> p c t i", i=4),
             )
             return grouped
 
-        def quantise(grouped, codes, scales):
-            nc.vector.quantize_mx(
-                out=codes.bitcast(FP8X4),
-                scales=scales,
-                in_=grouped[:].rearrange("p c t -> p (c t)"),
+        head_grouped = {}
+        head_codes = {}
+        head_scales = {}
+
+        def head_transpose(g):
+            grouped = stream.tile(
+                [P, HEAD_NODES * PACK], BF16, name="head_grouped", align_bytes=64
             )
+            grouped_words = grouped[:].bitcast(F32).rearrange("p (s r u) -> p s r u", r=P, u=2)
+            for h in range(HEAD_TILES // 2):
+                xt = xt_pool.tile([P, PLANES_PER_BANK, P], F32, name="xt")
+                for b in range(PLANES_PER_BANK):
+                    s, u = divmod(b, 2)
+                    words = a_head[g][:, 2 * h + s, :].bitcast(F32)
+                    nc.tensor.transpose(xt[:, b, :], words[:, u::2], ident[:])
+                nc.scalar.copy(
+                    out=grouped_words[:, 2 * h : 2 * h + 2],
+                    in_=xt[:].rearrange("p (s u) r -> p s r u", u=2),
+                )
+            head_grouped[g] = grouped
 
-        f_grouped = []
-        for g in range(A_PASSES):
-            f_grouped.append(regroup_features(f_raw[g], "f_grouped%d" % g))
-            if g >= 1:
-                quantise(f_grouped[g - 1], f_codes[:, g - 1, :], f_scales[:, g - 1, :])
-        quantise(f_grouped[A_PASSES - 1], f_codes[:, A_PASSES - 1, :], f_scales[:, A_PASSES - 1, :])
+        def head_quantise(g):
+            codes = stream.tile([P, HEAD_NODES], U32, name="head_codes", align_bytes=64)
+            scales = stream.tile([P, HEAD_NODES], U8, name="head_scales", align_bytes=64)
+            quantise(head_grouped[g][:], codes[:], scales[:])
+            head_codes[g] = codes
+            head_scales[g] = scales
 
+        head_agg = []
+
+        def head_multiply(g):
+            for t in range(FEAT_BLOCKS):
+                if g == 0:
+                    head_agg.append(
+                        bank_pool.tile([P, HEAD_NODES], F32, name="agg_t%d" % t, tag="bank%d" % t)
+                    )
+                block = slice(t * P, (t + 1) * P)
+                nc.tensor.matmul_mx(
+                    out=head_agg[t][:],
+                    lhsT=f_codes[:, g, block].bitcast(FP8X4),
+                    lhsT_scale=f_scales[:, g, block],
+                    rhs=head_codes[g][:].bitcast(FP8X4),
+                    rhs_scale=head_scales[g][:],
+                    start=(g == 0),
+                    stop=(g == A_PASSES - 1),
+                )
+
+        a_words = {}
         a_grouped = {}
         a_codes = {}
         a_scales = {}
@@ -133,6 +178,18 @@ def tile_net_pa_kernel(tc, A, features, Wg, bg, out):
         passes_per_bank = PLANES_PER_BANK // 2
         bank_columns = passes_per_bank * ROUND_NODES
 
+        def tiles_of(i):
+            first = HEAD_TILES + i * TILES_PER_ROUND
+            return range(first, first + TILES_PER_ROUND)
+
+        def order_words(j):
+            ordered = stream.tile([P, NODES // 2], F32, name="a_words", bufs=4)
+            nc.vector.tensor_copy(
+                out=ordered[:].rearrange("p (g u m) -> p g u m", u=2, m=P),
+                in_=a_rows[j][:].bitcast(F32).rearrange("p (g m u) -> p g u m", u=2, m=P),
+            )
+            a_words[j] = ordered
+
         def transpose_a(i):
             grouped = stream.tile(
                 [P, A_PASSES * ROUND_NODES * PACK], BF16, name="a_grouped", align_bytes=64
@@ -140,15 +197,18 @@ def tile_net_pa_kernel(tc, A, features, Wg, bg, out):
             grouped_words = grouped[:].bitcast(F32).rearrange(
                 "p (g s r u) -> p g s r u", g=A_PASSES, s=TILES_PER_ROUND, u=2
             )
-            for s in range(TILES_PER_ROUND):
-                words = a_rows[i * TILES_PER_ROUND + s][:].bitcast(F32)
-                for h in range(BANKS_PER_TILE):
+            for h in range(BANKS_PER_TILE):
+                for s, j in enumerate(tiles_of(i)):
                     xt = xt_pool.tile([P, PLANES_PER_BANK, P], F32, name="xt")
                     for b in range(PLANES_PER_BANK):
-                        g, u = divmod(h * PLANES_PER_BANK + b, 2)
-                        nc.tensor.transpose(
-                            xt[:, b, :], words[:, 2 * P * g + u : 2 * P * (g + 1) : 2], ident[:]
-                        )
+                        plane = h * PLANES_PER_BANK + b
+                        if j in a_words:
+                            words = a_words[j][:, plane * P : (plane + 1) * P]
+                        else:
+                            g, u = divmod(plane, 2)
+                            row = a_rows[j][:].bitcast(F32)
+                            words = row[:, 2 * P * g + u : 2 * P * (g + 1) : 2]
+                        nc.tensor.transpose(xt[:, b, :], words, ident[:])
                     nc.scalar.copy(
                         out=grouped_words[:, h * passes_per_bank : (h + 1) * passes_per_bank, s],
                         in_=xt[:].rearrange("p (g u) r -> p g r u", u=2),
@@ -159,18 +219,30 @@ def tile_net_pa_kernel(tc, A, features, Wg, bg, out):
             codes = stream.tile([P, A_PASSES * ROUND_NODES], U32, name="a_codes", align_bytes=64)
             scales = stream.tile([P, A_PASSES * ROUND_NODES], U8, name="a_scales", align_bytes=64)
             for h in range(BANKS_PER_TILE):
-                nc.vector.quantize_mx(
-                    out=codes[:, h * bank_columns : (h + 1) * bank_columns].bitcast(FP8X4),
-                    scales=scales[:, h * bank_columns : (h + 1) * bank_columns],
-                    in_=a_grouped[i][:, h * bank_columns * PACK : (h + 1) * bank_columns * PACK],
+                columns = slice(h * bank_columns, (h + 1) * bank_columns)
+                quantise(
+                    a_grouped[i][:, h * bank_columns * PACK : (h + 1) * bank_columns * PACK],
+                    codes[:, columns],
+                    scales[:, columns],
                 )
             a_codes[i] = codes
             a_scales[i] = scales
 
-        def aggregate(i):
+        def quantise_agg(grouped, width, first_tile):
+            codes = stream.tile([P, width], U32, name="agg_codes", align_bytes=64)
+            scales = stream.tile([P, width], U8, name="agg_scales", align_bytes=64)
+            quantise(grouped, codes[:], scales[:])
+            for s in range(width // P):
+                nodes = slice(s * P, (s + 1) * P)
+                agg_codes[first_tile + s] = codes[:, nodes]
+                agg_scales[first_tile + s] = scales[:, nodes]
+
+        def aggregate(i, between):
             grouped = stream.tile([P, ROUND_NODES, PACK], BF16, name="agg_grouped", align_bytes=64)
             for b in range(AGG_BANKS):
-                agg = agg_pool.tile([P, BLOCKS_PER_BANK, ROUND_NODES], F32, name="agg")
+                agg = bank_pool.tile(
+                    [P, BLOCKS_PER_BANK, ROUND_NODES], F32, name="agg", tag="bank%d" % b
+                )
                 for t in range(BLOCKS_PER_BANK):
                     block = (b * BLOCKS_PER_BANK + t) * P
                     for g in range(A_PASSES):
@@ -187,22 +259,20 @@ def tile_net_pa_kernel(tc, A, features, Wg, bg, out):
                     out=grouped[:, :, b * BLOCKS_PER_BANK : (b + 1) * BLOCKS_PER_BANK],
                     in_=agg[:].rearrange("p t n -> p n t"),
                 )
-            codes = stream.tile([P, ROUND_NODES], U32, name="agg_codes", align_bytes=64)
-            scales = stream.tile([P, ROUND_NODES], U8, name="agg_scales", align_bytes=64)
-            quantise(grouped, codes[:], scales[:])
-            agg_codes[i] = codes
-            agg_scales[i] = scales
+                if b == 0:
+                    between()
+            quantise_agg(grouped[:].rearrange("p n t -> p (n t)"), ROUND_NODES, tiles_of(i)[0])
 
         result = {}
 
         def project(j):
-            first = (j % TILES_PER_ROUND) * P
-            nodes = slice(first, first + P)
-            out_psum = out_pool.tile([P, FEAT], F32, name="out_psum")
+            out_psum = bank_pool.tile(
+                [P, FEAT], F32, name="out_psum", tag="bank%d" % (AGG_BANKS + j % OUT_BANKS)
+            )
             nc.tensor.matmul_mx(
                 out=out_psum[:],
-                lhsT=agg_codes[j // TILES_PER_ROUND][:, nodes].bitcast(FP8X4),
-                lhsT_scale=agg_scales[j // TILES_PER_ROUND][:, nodes],
+                lhsT=agg_codes[j].bitcast(FP8X4),
+                lhsT_scale=agg_scales[j],
                 rhs=w_codes[:].bitcast(FP8X4),
                 rhs_scale=w_scales[:],
                 start=True,
@@ -213,32 +283,81 @@ def tile_net_pa_kernel(tc, A, features, Wg, bg, out):
                 out=result[j][:], in0=out_psum[:], in1=bias[:], op=mybir.AluOpType.add
             )
 
-        def finish(j):
-            nc.vector.tensor_scalar_max(out=result[j][:], in0=result[j][:], scalar1=0.0)
+        def store(j):
             nc.sync.dma_start(out=out[j * P : (j + 1) * P, :], in_=result[j][:])
 
-        def tiles_of(i):
-            return range(i * TILES_PER_ROUND, (i + 1) * TILES_PER_ROUND)
+        def relu_on_vector(j):
+            nc.vector.tensor_scalar_max(out=result[j][:], in0=result[j][:], scalar1=0.0)
+            store(j)
 
-        transpose_a(0)
+        def relu_on_scalar(j):
+            nc.scalar.activation(
+                out=result[j][:], in_=result[j][:], func=mybir.ActivationFunctionType.Relu
+            )
+            store(j)
+
+        head_transpose(0)
+        f_grouped = regroup_features(0)
+        head_transpose(1)
+        for g in range(A_PASSES):
+            head_quantise(g)
+            quantise(f_grouped[:], f_codes[:, g, :], f_scales[:, g, :])
+            if g + 1 < A_PASSES:
+                f_grouped = regroup_features(g + 1)
+            head_multiply(g)
+            if g + 2 < A_PASSES:
+                head_transpose(g + 2)
+            if g == A_PASSES - 2:
+                transpose_a(0)
+        w_grouped = regroup_weights()
         quantise_a(0)
-        for i in range(1, AHEAD):
-            transpose_a(i)
-        bias_psum = out_pool.tile([P, FEAT], F32, name="bias_psum", tag="out_psum")
+        quantise(w_grouped[:], w_codes[:], w_scales[:])
+        agg_rounded = keep.tile([P, FEAT_BLOCKS, HEAD_NODES], BF16)
+        for t in range(FEAT_BLOCKS):
+            nc.scalar.copy(out=agg_rounded[:, t, :], in_=head_agg[t][:])
+        transpose_a(1)
+        bias_psum = bank_pool.tile([P, FEAT], F32, name="bias_psum", tag="bank2")
         nc.tensor.matmul(out=bias_psum[:], lhsT=ones[:], rhs=bias_row[:], start=True, stop=True)
-        bias = keep.tile([P, FEAT], F32)
         nc.scalar.copy(out=bias[:], in_=bias_psum[:])
-        quantise(regroup_weights(w_raw, "w_grouped"), w_codes[:], w_scales[:])
+        for h in range(HEAD_TILES // TILES_PER_ROUND):
+            grouped = stream.tile([P, ROUND_NODES, PACK], BF16, name="agg_grouped", align_bytes=64)
+            nodes = slice(h * ROUND_NODES, (h + 1) * ROUND_NODES)
+            nc.vector.tensor_copy(
+                out=grouped[:], in_=agg_rounded[:, :, nodes].rearrange("p t n -> p n t")
+            )
+            quantise_agg(
+                grouped[:].rearrange("p n t -> p (n t)"), ROUND_NODES, h * TILES_PER_ROUND
+            )
 
-        for i in range(ROUNDS + 1):
+        waiting = list(range(HEAD_TILES))
+        ordered_ahead = [j for j in range(HEAD_TILES + 2 * 2, NODE_TILES) if j % 2 in (0, 1)]
+        for i in range(ROUNDS):
             if i + 1 < ROUNDS:
                 quantise_a(i + 1)
-            if i < ROUNDS:
-                aggregate(i)
-            if i >= 1:
-                for j in tiles_of(i - 1):
+            count = 3 if (1, 3)[0] <= i < (1, 3)[1] else 2
+            now = waiting[:count]
+            waiting = waiting[count:] + list(tiles_of(i))
+
+            def between():
+                for j in now[:2]:
                     project(j)
-                for j in tiles_of(i - 1):
-                    finish(j)
-            if i + AHEAD < ROUNDS:
-                transpose_a(i + AHEAD)
+                for j in now[:2]:
+                    if j % 2 == 0 or False:
+                        relu_on_vector(j)
+                if i + 3 < ROUNDS:
+                    for j in tiles_of(i + 3):
+                        if j in ordered_ahead:
+                            order_words(j)
+
+            aggregate(i, between)
+            for j in now[2:]:
+                project(j)
+                relu_on_vector(j)
+            if i + 2 < ROUNDS:
+                transpose_a(i + 2)
+            for j in now[:2]:
+                if not (j % 2 == 0 or False):
+                    relu_on_scalar(j)
+        for j in waiting:
+            project(j)
+            relu_on_vector(j)

@@ -190,30 +190,30 @@ def tile_net_pa_kernel(tc, A, features, Wg, bg, out):
             )
             a_words[j] = ordered
 
-        def transpose_a(i):
-            grouped = stream.tile(
-                [P, A_PASSES * ROUND_NODES * PACK], BF16, name="a_grouped", align_bytes=64
-            )
-            grouped_words = grouped[:].bitcast(F32).rearrange(
+        def transpose_a(i, s):
+            if s == 0:
+                a_grouped[i] = stream.tile(
+                    [P, A_PASSES * ROUND_NODES * PACK], BF16, name="a_grouped", align_bytes=64
+                )
+            grouped_words = a_grouped[i][:].bitcast(F32).rearrange(
                 "p (g s r u) -> p g s r u", g=A_PASSES, s=TILES_PER_ROUND, u=2
             )
+            j = tiles_of(i)[s]
             for h in range(BANKS_PER_TILE):
-                for s, j in enumerate(tiles_of(i)):
-                    xt = xt_pool.tile([P, PLANES_PER_BANK, P], F32, name="xt")
-                    for b in range(PLANES_PER_BANK):
-                        plane = h * PLANES_PER_BANK + b
-                        if j in a_words:
-                            words = a_words[j][:, plane * P : (plane + 1) * P]
-                        else:
-                            g, u = divmod(plane, 2)
-                            row = a_rows[j][:].bitcast(F32)
-                            words = row[:, 2 * P * g + u : 2 * P * (g + 1) : 2]
-                        nc.tensor.transpose(xt[:, b, :], words, ident[:])
-                    nc.scalar.copy(
-                        out=grouped_words[:, h * passes_per_bank : (h + 1) * passes_per_bank, s],
-                        in_=xt[:].rearrange("p (g u) r -> p g r u", u=2),
-                    )
-            a_grouped[i] = grouped
+                xt = xt_pool.tile([P, PLANES_PER_BANK, P], F32, name="xt")
+                for b in range(PLANES_PER_BANK):
+                    plane = h * PLANES_PER_BANK + b
+                    if j in a_words:
+                        words = a_words[j][:, plane * P : (plane + 1) * P]
+                    else:
+                        g, u = divmod(plane, 2)
+                        row = a_rows[j][:].bitcast(F32)
+                        words = row[:, 2 * P * g + u : 2 * P * (g + 1) : 2]
+                    nc.tensor.transpose(xt[:, b, :], words, ident[:])
+                nc.scalar.copy(
+                    out=grouped_words[:, h * passes_per_bank : (h + 1) * passes_per_bank, s],
+                    in_=xt[:].rearrange("p (g u) r -> p g r u", u=2),
+                )
 
         def quantise_a(i):
             codes = stream.tile([P, A_PASSES * ROUND_NODES], U32, name="a_codes", align_bytes=64)
@@ -263,6 +263,28 @@ def tile_net_pa_kernel(tc, A, features, Wg, bg, out):
                     between()
             quantise_agg(grouped[:].rearrange("p n t -> p (n t)"), ROUND_NODES, tiles_of(i)[0])
 
+        def aggregate_tiles(i, between):
+            for s, j in enumerate(tiles_of(i)):
+                grouped = stream.tile([P, P, PACK], BF16, name="tile_grouped", align_bytes=64)
+                agg = bank_pool.tile([P, FEAT_BLOCKS, P], F32, name="agg", tag="bank%d" % s)
+                for t in range(FEAT_BLOCKS):
+                    block = t * P
+                    for g in range(A_PASSES):
+                        first = g * ROUND_NODES + s * P
+                        nc.tensor.matmul_mx(
+                            out=agg[:, t, :],
+                            lhsT=f_codes[:, g, block : block + P].bitcast(FP8X4),
+                            lhsT_scale=f_scales[:, g, block : block + P],
+                            rhs=a_codes[i][:, first : first + P].bitcast(FP8X4),
+                            rhs_scale=a_scales[i][:, first : first + P],
+                            start=(g == 0),
+                            stop=(g == A_PASSES - 1),
+                        )
+                nc.scalar.copy(out=grouped[:], in_=agg[:].rearrange("p t n -> p n t"))
+                if s == 0:
+                    between()
+                quantise_agg(grouped[:].rearrange("p n t -> p (n t)"), P, j)
+
         result = {}
 
         def project(j):
@@ -296,6 +318,34 @@ def tile_net_pa_kernel(tc, A, features, Wg, bg, out):
             )
             store(j)
 
+        def project_last(j):
+            out_psum = bank_pool.tile(
+                [P, FEAT], F32, name="out_psum", tag="bank%d" % (AGG_BANKS + j % OUT_BANKS)
+            )
+            nc.tensor.matmul_mx(
+                out=out_psum[:],
+                lhsT=agg_codes[j].bitcast(FP8X4),
+                lhsT_scale=agg_scales[j],
+                rhs=w_codes[:].bitcast(FP8X4),
+                rhs_scale=w_scales[:],
+                start=True,
+                stop=True,
+            )
+            half = FEAT // 2
+            for h in range(2):
+                columns = slice(h * half, (h + 1) * half)
+                part = result_pool.tile([P, half], F32, name="part%d" % h, bufs=1)
+                nc.vector.tensor_tensor(
+                    out=part[:], in0=out_psum[:, columns], in1=bias[:, columns], op=mybir.AluOpType.add
+                )
+                if h == 0:
+                    nc.scalar.activation(
+                        out=part[:], in_=part[:], func=mybir.ActivationFunctionType.Relu
+                    )
+                else:
+                    nc.vector.tensor_scalar_max(out=part[:], in0=part[:], scalar1=0.0)
+                nc.sync.dma_start(out=out[j * P : (j + 1) * P, columns], in_=part[:])
+
         head_transpose(0)
         f_grouped = regroup_features(0)
         head_transpose(1)
@@ -308,14 +358,16 @@ def tile_net_pa_kernel(tc, A, features, Wg, bg, out):
             if g + 2 < A_PASSES:
                 head_transpose(g + 2)
             if g == A_PASSES - 2:
-                transpose_a(0)
+                transpose_a(0, 0)
         w_grouped = regroup_weights()
+        transpose_a(0, 1)
         quantise_a(0)
         quantise(w_grouped[:], w_codes[:], w_scales[:])
         agg_rounded = keep.tile([P, FEAT_BLOCKS, HEAD_NODES], BF16)
         for t in range(FEAT_BLOCKS):
             nc.scalar.copy(out=agg_rounded[:, t, :], in_=head_agg[t][:])
-        transpose_a(1)
+        transpose_a(1, 0)
+        transpose_a(1, 1)
         bias_psum = bank_pool.tile([P, FEAT], F32, name="bias_psum", tag="bank2")
         nc.tensor.matmul(out=bias_psum[:], lhsT=ones[:], rhs=bias_row[:], start=True, stop=True)
         nc.scalar.copy(out=bias[:], in_=bias_psum[:])
@@ -339,25 +391,34 @@ def tile_net_pa_kernel(tc, A, features, Wg, bg, out):
             waiting = waiting[count:] + list(tiles_of(i))
 
             def between():
+                if i + 2 < ROUNDS and (True):
+                    transpose_a(i + 2, 0)
                 for j in now[:2]:
                     project(j)
                 for j in now[:2]:
-                    if j % 2 == 0 or False:
+                    if j % 2 == 0:
                         relu_on_vector(j)
                 if i + 3 < ROUNDS:
                     for j in tiles_of(i + 3):
                         if j in ordered_ahead:
                             order_words(j)
 
-            aggregate(i, between)
+            if i < ROUNDS - 1:
+                aggregate(i, between)
+            else:
+                aggregate_tiles(i, between)
             for j in now[2:]:
                 project(j)
                 relu_on_vector(j)
             if i + 2 < ROUNDS:
-                transpose_a(i + 2)
+                if not (True):
+                    transpose_a(i + 2, 0)
+                transpose_a(i + 2, 1)
             for j in now[:2]:
-                if not (j % 2 == 0 or False):
+                if not (j % 2 == 0):
                     relu_on_scalar(j)
-        for j in waiting:
+        for j in waiting[:-1]:
             project(j)
             relu_on_vector(j)
+        for j in waiting[-1:]:
+            project_last(j)

@@ -396,14 +396,14 @@ def tile_net_pa_kernel(tc, A, features, Wg, bg, out):
                 for j in now[:2]:
                     project(j)
                 for j in now[:2]:
-                    if j % 2 == 0:
+                    if False:
                         relu_on_vector(j)
                 if i + 3 < ROUNDS:
                     for j in tiles_of(i + 3):
                         if j in ordered_ahead:
                             order_words(j)
 
-            if i < ROUNDS - 1:
+            if i < ROUNDS - 6:
                 aggregate(i, between)
             else:
                 aggregate_tiles(i, between)
@@ -415,7 +415,7 @@ def tile_net_pa_kernel(tc, A, features, Wg, bg, out):
                     transpose_a(i + 2, 0)
                 transpose_a(i + 2, 1)
             for j in now[:2]:
-                if not (j % 2 == 0):
+                if not (False):
                     relu_on_scalar(j)
         for j in waiting[:-1]:
             project(j)

@@ -78,11 +78,11 @@ def tile_net_pa_kernel(tc, A, features, Wg, bg, out):
             a_rows[j] = a_pool.tile([P, NODES], BF16, name="a_rows%d" % j, tag="a_rows")
             nc.sync.dma_start(out=a_rows[j][:], in_=A[j * P : (j + 1) * P, :])
 
-        for j in range(HEAD_TILES, HEAD_TILES + TILES_PER_ROUND):
+        for j in range(HEAD_TILES, HEAD_TILES + 2 * TILES_PER_ROUND):
             load_a(j)
         w_raw = raw_pool.tile([P, PACK, FEAT], BF16, name="w_raw", tag="raw")
         nc.sync.dma_start(out=w_raw[:], in_=Wg.rearrange("(p t) n -> p t n", t=PACK))
-        for j in range(HEAD_TILES + TILES_PER_ROUND, NODE_TILES):
+        for j in range(HEAD_TILES + 2 * TILES_PER_ROUND, NODE_TILES):
             load_a(j)
 
         ident = keep.tile([P, P], F32)
@@ -229,8 +229,8 @@ def tile_net_pa_kernel(tc, A, features, Wg, bg, out):
             a_scales[i] = scales
 
         def quantise_agg(grouped, width, first_tile):
-            codes = stream.tile([P, width], U32, name="agg_codes", align_bytes=64)
-            scales = stream.tile([P, width], U8, name="agg_scales", align_bytes=64)
+            codes = stream.tile([P, width], U32, name="agg_codes", bufs=8, align_bytes=64)
+            scales = stream.tile([P, width], U8, name="agg_scales", bufs=8, align_bytes=64)
             quantise(grouped, codes[:], scales[:])
             for s in range(width // P):
                 nodes = slice(s * P, (s + 1) * P)
@@ -354,24 +354,32 @@ def tile_net_pa_kernel(tc, A, features, Wg, bg, out):
             quantise(f_grouped[:], f_codes[:, g, :], f_scales[:, g, :])
             if g + 1 < A_PASSES:
                 f_grouped = regroup_features(g + 1)
+            if g == A_PASSES - 1:
+                transpose_a(0, 0)
+                transpose_a(0, 1)
             head_multiply(g)
             if g + 2 < A_PASSES:
                 head_transpose(g + 2)
-            if g == A_PASSES - 2:
-                transpose_a(0, 0)
+        for j in tiles_of(1):
+            order_words(j)
         w_grouped = regroup_weights()
-        transpose_a(0, 1)
         quantise_a(0)
-        quantise(w_grouped[:], w_codes[:], w_scales[:])
         agg_rounded = keep.tile([P, FEAT_BLOCKS, HEAD_NODES], BF16)
         for t in range(FEAT_BLOCKS):
-            nc.scalar.copy(out=agg_rounded[:, t, :], in_=head_agg[t][:])
+            if t < FEAT_BLOCKS - 0:
+                nc.scalar.copy(out=agg_rounded[:, t, :], in_=head_agg[t][:])
+            else:
+                nc.vector.tensor_copy(out=agg_rounded[:, t, :], in_=head_agg[t][:])
+        quantise(w_grouped[:], w_codes[:], w_scales[:])
         transpose_a(1, 0)
         transpose_a(1, 1)
-        bias_psum = bank_pool.tile([P, FEAT], F32, name="bias_psum", tag="bank2")
-        nc.tensor.matmul(out=bias_psum[:], lhsT=ones[:], rhs=bias_row[:], start=True, stop=True)
-        nc.scalar.copy(out=bias[:], in_=bias_psum[:])
-        for h in range(HEAD_TILES // TILES_PER_ROUND):
+
+        def spread_bias():
+            bias_psum = bank_pool.tile([P, FEAT], F32, name="bias_psum", tag="bank2")
+            nc.tensor.matmul(out=bias_psum[:], lhsT=ones[:], rhs=bias_row[:], start=True, stop=True)
+            nc.vector.tensor_copy(out=bias[:], in_=bias_psum[:])
+
+        def head_codes_of(h):
             grouped = stream.tile([P, ROUND_NODES, PACK], BF16, name="agg_grouped", align_bytes=64)
             nodes = slice(h * ROUND_NODES, (h + 1) * ROUND_NODES)
             nc.vector.tensor_copy(
@@ -382,17 +390,22 @@ def tile_net_pa_kernel(tc, A, features, Wg, bg, out):
             )
 
         waiting = list(range(HEAD_TILES))
-        ordered_ahead = [j for j in range(HEAD_TILES + 2 * 2, NODE_TILES) if j % 2 in (0, 1)]
+        ordered_ahead = [10, 11, 12, 13, 14, 15]
+        counts = [0, 3, 3, 3, 3, 2]
         for i in range(ROUNDS):
+            if i < 2:
+                head_codes_of(i)
             if i + 1 < ROUNDS:
                 quantise_a(i + 1)
-            count = 3 if (1, 3)[0] <= i < (1, 3)[1] else 2
-            now = waiting[:count]
-            waiting = waiting[count:] + list(tiles_of(i))
+            now = waiting[: counts[i]]
+            waiting = waiting[counts[i] :] + list(tiles_of(i))
+            alternate = i + 2 < 3
 
             def between():
-                if i + 2 < ROUNDS and (True):
+                if i + 2 < ROUNDS and alternate:
                     transpose_a(i + 2, 0)
+                if i == 0:
+                    spread_bias()
                 for j in now[:2]:
                     project(j)
                 for j in now[:2]:
@@ -411,7 +424,7 @@ def tile_net_pa_kernel(tc, A, features, Wg, bg, out):
                 project(j)
                 relu_on_vector(j)
             if i + 2 < ROUNDS:
-                if not (True):
+                if not alternate:
                     transpose_a(i + 2, 0)
                 transpose_a(i + 2, 1)
             for j in now[:2]:
@@ -420,5 +433,4 @@ def tile_net_pa_kernel(tc, A, features, Wg, bg, out):
         for j in waiting[:-1]:
             project(j)
             relu_on_vector(j)
-        for j in waiting[-1:]:
-            project_last(j)
+        project_last(waiting[-1])

@@ -152,8 +152,8 @@ def tile_net_pa_kernel(tc, A, features, Wg, bg, out):
 
         head_agg = []
 
-        def head_multiply(g):
-            for t in range(FEAT_BLOCKS):
+        def head_multiply(g, blocks=range(FEAT_BLOCKS)):
+            for t in blocks:
                 if g == 0:
                     head_agg.append(
                         bank_pool.tile([P, HEAD_NODES], F32, name="agg_t%d" % t, tag="bank%d" % t)
@@ -346,20 +346,30 @@ def tile_net_pa_kernel(tc, A, features, Wg, bg, out):
                     nc.vector.tensor_scalar_max(out=part[:], in0=part[:], scalar1=0.0)
                 nc.sync.dma_start(out=out[j * P : (j + 1) * P, columns], in_=part[:])
 
+        warm = bank_pool.tile([P, FEAT], F32, name="warm", tag="bank3")
+        zeros = keep.tile([P, FEAT], BF16)
+        nc.gpsimd.memset(zeros[:], 0.0)
+        for i in range(0):
+            nc.tensor.matmul(out=warm[:], lhsT=zeros[:, :P], rhs=zeros[:], start=True, stop=True)
         head_transpose(0)
+        for i in range(0):
+            nc.tensor.matmul(out=warm[:], lhsT=zeros[:, :P], rhs=zeros[:], start=True, stop=True)
         f_grouped = regroup_features(0)
         head_transpose(1)
+        for i in range(2):
+            nc.tensor.matmul(out=warm[:], lhsT=zeros[:, :P], rhs=zeros[:], start=True, stop=True)
         for g in range(A_PASSES):
             head_quantise(g)
             quantise(f_grouped[:], f_codes[:, g, :], f_scales[:, g, :])
             if g + 1 < A_PASSES:
                 f_grouped = regroup_features(g + 1)
-            if g == A_PASSES - 1:
-                transpose_a(0, 0)
-                transpose_a(0, 1)
-            head_multiply(g)
             if g + 2 < A_PASSES:
                 head_transpose(g + 2)
+            if g == A_PASSES - 2:
+                transpose_a(0, 0)
+            if g == A_PASSES - 1:
+                transpose_a(0, 1)
+            head_multiply(g)
         for j in tiles_of(1):
             order_words(j)
         w_grouped = regroup_weights()
@@ -390,7 +400,7 @@ def tile_net_pa_kernel(tc, A, features, Wg, bg, out):
             )
 
         waiting = list(range(HEAD_TILES))
-        ordered_ahead = [10, 11, 12, 13, 14, 15]
+        ordered_ahead = [11, 13, 15]
         counts = [0, 3, 3, 3, 3, 2]
         for i in range(ROUNDS):
             if i < 2:
@@ -399,7 +409,7 @@ def tile_net_pa_kernel(tc, A, features, Wg, bg, out):
                 quantise_a(i + 1)
             now = waiting[: counts[i]]
             waiting = waiting[counts[i] :] + list(tiles_of(i))
-            alternate = i + 2 < 3
+            alternate = True
 
             def between():
                 if i + 2 < ROUNDS and alternate:
@@ -416,7 +426,7 @@ def tile_net_pa_kernel(tc, A, features, Wg, bg, out):
                         if j in ordered_ahead:
                             order_words(j)
 
-            if i < ROUNDS - 6:
+            if i < ROUNDS - 2:
                 aggregate(i, between)
             else:
                 aggregate_tiles(i, between)

from contextlib import ExitStack

import concourse.mybir as mybir
from concourse.masks import make_identity

F32 = mybir.dt.float32
BF16 = mybir.dt.bfloat16
U32 = mybir.dt.uint32
U8 = mybir.dt.uint8
FP8X4 = mybir.dt.float8_e4m3fn_x4

P = 128
PACK = 4
K_PASS = P * PACK
NODES = 2048
FEAT = 512
A_PASSES = NODES // K_PASS
FEAT_BLOCKS = FEAT // P
NODE_TILES = NODES // P
HEAD_TILES = 4
HEAD_NODES = HEAD_TILES * P
TILES_PER_ROUND = 2
ROUND_NODES = TILES_PER_ROUND * P
ROUNDS = (NODE_TILES - HEAD_TILES) // TILES_PER_ROUND
PLANES_PER_BANK = 4
BANKS_PER_TILE = NODES // 2 // P // PLANES_PER_BANK
XT_BANKS = 4
AGG_BANKS = 2
OUT_BANKS = 2
BLOCKS_PER_BANK = FEAT_BLOCKS // AGG_BANKS

FLOPS = 2 * NODES * NODES * FEAT + 2 * NODES * FEAT * FEAT


def tile_net_pa_kernel(tc, A, features, Wg, bg, out):
    nc = tc.nc
    with ExitStack() as ctx:
        keep = ctx.enter_context(tc.tile_pool(name="keep", bufs=1))
        a_pool = ctx.enter_context(
            tc.tile_pool(name="a_rows", bufs=NODE_TILES - HEAD_TILES)
        )
        raw_pool = ctx.enter_context(tc.tile_pool(name="raw", bufs=A_PASSES + 1))
        head_pool = ctx.enter_context(tc.tile_pool(name="head", bufs=A_PASSES))
        regroup_pool = ctx.enter_context(tc.tile_pool(name="regroup", bufs=2))
        stream = ctx.enter_context(tc.tile_pool(name="stream", bufs=3))
        result_pool = ctx.enter_context(tc.tile_pool(name="result", bufs=8))
        xt_pool = ctx.enter_context(tc.psum_pool(name="xt", bufs=XT_BANKS))
        bank_pool = ctx.enter_context(tc.psum_pool(name="banks", bufs=1))
        ctx.enter_context(tc.manual_schedule())

        bias_row = keep.tile([P, FEAT], BF16)
        nc.vector.memset(bias_row[:], 0.0)
        nc.scalar.dma_start(out=bias_row[0:1, :], in_=bg.unsqueeze(0))

        a_head = []
        f_raw = []
        for g in range(A_PASSES):
            rows = head_pool.tile([P, HEAD_TILES, K_PASS], BF16, name="a_head%d" % g, tag="a_head")
            nc.sync.dma_start(
                out=rows[:],
                in_=A[0:HEAD_NODES, g * K_PASS : (g + 1) * K_PASS].rearrange(
                    "(s p) k -> p s k", p=P
                ),
            )
            a_head.append(rows)
            raw = raw_pool.tile([P, PACK, FEAT], BF16, name="f_raw%d" % g, tag="raw")
            nc.sync.dma_start(
                out=raw[:],
                in_=features[g * K_PASS : (g + 1) * K_PASS, :].rearrange(
                    "(p j) c -> p j c", j=PACK
                ),
            )
            f_raw.append(raw)

        a_rows = {}

        def load_a(j):
            a_rows[j] = a_pool.tile([P, NODES], BF16, name="a_rows%d" % j, tag="a_rows")
            nc.sync.dma_start(out=a_rows[j][:], in_=A[j * P : (j + 1) * P, :])

        for j in range(HEAD_TILES, HEAD_TILES + 2 * TILES_PER_ROUND):
            load_a(j)
        w_raw = raw_pool.tile([P, PACK, FEAT], BF16, name="w_raw", tag="raw")
        nc.sync.dma_start(out=w_raw[:], in_=Wg.rearrange("(p t) n -> p t n", t=PACK))
        for j in range(HEAD_TILES + 2 * TILES_PER_ROUND, NODE_TILES):
            load_a(j)

        ident = keep.tile([P, P], F32)
        make_identity(nc, ident[:])
        ones = keep.tile([P, P], BF16)
        nc.vector.memset(ones[:], 1.0)
        bias = keep.tile([P, FEAT], F32)

        f_codes = keep.tile([P, A_PASSES, FEAT], U32, align_bytes=64)
        f_scales = keep.tile([P, A_PASSES, FEAT], U8, align_bytes=64)
        w_codes = keep.tile([P, FEAT], U32, align_bytes=64)
        w_scales = keep.tile([P, FEAT], U8, align_bytes=64)

        def quantise(grouped, codes, scales):
            nc.vector.quantize_mx(out=codes.bitcast(FP8X4), scales=scales, in_=grouped)

        V_BLOCKS = 3

        def regroup_features(g):
            grouped = regroup_pool.tile(
                [P, FEAT * PACK], BF16, name="f_grouped%d" % g, tag="grouped", align_bytes=64
            )
            columns = f_raw[g][:].rearrange("p j (m t) -> p t m j", t=FEAT_BLOCKS)
            blocks = grouped[:].rearrange("p (t m j) -> p t m j", t=FEAT_BLOCKS, j=PACK)
            nc.vector.tensor_copy(out=blocks[:, :2], in_=columns[:, :2])
            nc.vector.tensor_copy(out=blocks[:, 2], in_=columns[:, 2])
            nc.scalar.copy(out=blocks[:, V_BLOCKS], in_=columns[:, V_BLOCKS])
            return grouped

        def regroup_weights():
            grouped = regroup_pool.tile(
                [P, FEAT * PACK], BF16, name="w_grouped", tag="grouped", align_bytes=64
            )
            nc.vector.tensor_copy(
                out=grouped[:].rearrange("p (c i t) -> p c t i", i=4, t=PACK),
                in_=w_raw[:].rearrange("p t (c i) -> p c t i", i=4),
            )
            return grouped

        head_grouped = {}
        head_codes = {}
        head_scales = {}

        def head_transpose(g):
            grouped = stream.tile(
                [P, HEAD_NODES * PACK], BF16, name="head_grouped", align_bytes=64
            )
            grouped_words = grouped[:].bitcast(F32).rearrange("p (s r u) -> p s r u", r=P, u=2)
            for h in range(HEAD_TILES // 2):
                xt = xt_pool.tile([P, PLANES_PER_BANK, P], F32, name="xt")
                for b in range(PLANES_PER_BANK):
                    s, u = divmod(b, 2)
                    words = a_head[g][:, 2 * h + s, :].bitcast(F32)
                    nc.tensor.transpose(xt[:, b, :], words[:, u::2], ident[:])
                nc.scalar.copy(
                    out=grouped_words[:, 2 * h : 2 * h + 2],
                    in_=xt[:].rearrange("p (s u) r -> p s r u", u=2),
                )
            head_grouped[g] = grouped

        def head_quantise(g):
            codes = stream.tile([P, HEAD_NODES], U32, name="head_codes", align_bytes=64)
            scales = stream.tile([P, HEAD_NODES], U8, name="head_scales", align_bytes=64)
            quantise(head_grouped[g][:], codes[:], scales[:])
            head_codes[g] = codes
            head_scales[g] = scales

        head_agg = []

        def head_multiply(g, blocks=range(FEAT_BLOCKS)):
            for t in blocks:
                if g == 0:
                    head_agg.append(
                        bank_pool.tile([P, HEAD_NODES], F32, name="agg_t%d" % t, tag="bank%d" % t)
                    )
                block = slice(t * P, (t + 1) * P)
                nc.tensor.matmul_mx(
                    out=head_agg[t][:],
                    lhsT=f_codes[:, g, block].bitcast(FP8X4),
                    lhsT_scale=f_scales[:, g, block],
                    rhs=head_codes[g][:].bitcast(FP8X4),
                    rhs_scale=head_scales[g][:],
                    start=(g == 0),
                    stop=(g == A_PASSES - 1),
                )

        a_words = {}
        a_grouped = {}
        a_codes = {}
        a_scales = {}
        agg_codes = {}
        agg_scales = {}
        passes_per_bank = PLANES_PER_BANK // 2
        bank_columns = passes_per_bank * ROUND_NODES

        def tiles_of(i):
            first = HEAD_TILES + i * TILES_PER_ROUND
            return range(first, first + TILES_PER_ROUND)

        def order_words(j):
            ordered = stream.tile([P, NODES // 2], F32, name="a_words", bufs=4)
            nc.vector.tensor_copy(
                out=ordered[:].rearrange("p (g u m) -> p g u m", u=2, m=P),
                in_=a_rows[j][:].bitcast(F32).rearrange("p (g m u) -> p g u m", u=2, m=P),
            )
            a_words[j] = ordered

        def transpose_a(i, s):
            if s == 0:
                a_grouped[i] = stream.tile(
                    [P, A_PASSES * ROUND_NODES * PACK], BF16, name="a_grouped", align_bytes=64
                )
            grouped_words = a_grouped[i][:].bitcast(F32).rearrange(
                "p (g s r u) -> p g s r u", g=A_PASSES, s=TILES_PER_ROUND, u=2
            )
            j = tiles_of(i)[s]
            for h in range(BANKS_PER_TILE):
                xt = xt_pool.tile([P, PLANES_PER_BANK, P], F32, name="xt")
                for b in range(PLANES_PER_BANK):
                    plane = h * PLANES_PER_BANK + b
                    if j in a_words:
                        words = a_words[j][:, plane * P : (plane + 1) * P]
                    else:
                        g, u = divmod(plane, 2)
                        row = a_rows[j][:].bitcast(F32)
                        words = row[:, 2 * P * g + u : 2 * P * (g + 1) : 2]
                    nc.tensor.transpose(xt[:, b, :], words, ident[:])
                nc.scalar.copy(
                    out=grouped_words[:, h * passes_per_bank : (h + 1) * passes_per_bank, s],
                    in_=xt[:].rearrange("p (g u) r -> p g r u", u=2),
                )

        def quantise_a(i):
            codes = stream.tile([P, A_PASSES * ROUND_NODES], U32, name="a_codes", align_bytes=64)
            scales = stream.tile([P, A_PASSES * ROUND_NODES], U8, name="a_scales", align_bytes=64)
            for h in range(BANKS_PER_TILE):
                columns = slice(h * bank_columns, (h + 1) * bank_columns)
                quantise(
                    a_grouped[i][:, h * bank_columns * PACK : (h + 1) * bank_columns * PACK],
                    codes[:, columns],
                    scales[:, columns],
                )
            a_codes[i] = codes
            a_scales[i] = scales

        def quantise_agg(grouped, width, first_tile):
            codes = stream.tile([P, width], U32, name="agg_codes", bufs=8, align_bytes=64)
            scales = stream.tile([P, width], U8, name="agg_scales", bufs=8, align_bytes=64)
            quantise(grouped, codes[:], scales[:])
            for s in range(width // P):
                nodes = slice(s * P, (s + 1) * P)
                agg_codes[first_tile + s] = codes[:, nodes]
                agg_scales[first_tile + s] = scales[:, nodes]

        def aggregate(i, between):
            grouped = stream.tile([P, ROUND_NODES, PACK], BF16, name="agg_grouped", align_bytes=64)
            for b in range(AGG_BANKS):
                agg = bank_pool.tile(
                    [P, BLOCKS_PER_BANK, ROUND_NODES], F32, name="agg", tag="bank%d" % b
                )
                for t in range(BLOCKS_PER_BANK):
                    block = (b * BLOCKS_PER_BANK + t) * P
                    for g in range(A_PASSES):
                        nc.tensor.matmul_mx(
                            out=agg[:, t, :],
                            lhsT=f_codes[:, g, block : block + P].bitcast(FP8X4),
                            lhsT_scale=f_scales[:, g, block : block + P],
                            rhs=a_codes[i][:, g * ROUND_NODES : (g + 1) * ROUND_NODES].bitcast(FP8X4),
                            rhs_scale=a_scales[i][:, g * ROUND_NODES : (g + 1) * ROUND_NODES],
                            start=(g == 0),
                            stop=(g == A_PASSES - 1),
                        )
                nc.scalar.copy(
                    out=grouped[:, :, b * BLOCKS_PER_BANK : (b + 1) * BLOCKS_PER_BANK],
                    in_=agg[:].rearrange("p t n -> p n t"),
                )
                if b == 0:
                    between()
            quantise_agg(grouped[:].rearrange("p n t -> p (n t)"), ROUND_NODES, tiles_of(i)[0])

        def aggregate_tiles(i, between):
            for s, j in enumerate(tiles_of(i)):
                grouped = stream.tile([P, P, PACK], BF16, name="tile_grouped", align_bytes=64)
                agg = bank_pool.tile([P, FEAT_BLOCKS, P], F32, name="agg", tag="bank%d" % s)
                for t in range(FEAT_BLOCKS):
                    block = t * P
                    for g in range(A_PASSES):
                        first = g * ROUND_NODES + s * P
                        nc.tensor.matmul_mx(
                            out=agg[:, t, :],
                            lhsT=f_codes[:, g, block : block + P].bitcast(FP8X4),
                            lhsT_scale=f_scales[:, g, block : block + P],
                            rhs=a_codes[i][:, first : first + P].bitcast(FP8X4),
                            rhs_scale=a_scales[i][:, first : first + P],
                            start=(g == 0),
                            stop=(g == A_PASSES - 1),
                        )
                nc.scalar.copy(out=grouped[:], in_=agg[:].rearrange("p t n -> p n t"))
                if s == 0:
                    between()
                quantise_agg(grouped[:].rearrange("p n t -> p (n t)"), P, j)

        result = {}

        def project(j):
            out_psum = bank_pool.tile(
                [P, FEAT], F32, name="out_psum", tag="bank%d" % (AGG_BANKS + j % OUT_BANKS)
            )
            nc.tensor.matmul_mx(
                out=out_psum[:],
                lhsT=agg_codes[j].bitcast(FP8X4),
                lhsT_scale=agg_scales[j],
                rhs=w_codes[:].bitcast(FP8X4),
                rhs_scale=w_scales[:],
                start=True,
                stop=True,
            )
            result[j] = result_pool.tile([P, FEAT], F32, name="result")
            nc.vector.tensor_tensor(
                out=result[j][:], in0=out_psum[:], in1=bias[:], op=mybir.AluOpType.add
            )

        def store(j):
            nc.sync.dma_start(out=out[j * P : (j + 1) * P, :], in_=result[j][:])

        def relu_on_vector(j):
            nc.vector.tensor_scalar_max(out=result[j][:], in0=result[j][:], scalar1=0.0)
            store(j)

        def relu_on_scalar(j):
            nc.scalar.activation(
                out=result[j][:], in_=result[j][:], func=mybir.ActivationFunctionType.Relu
            )
            store(j)

        def project_last(j):
            out_psum = bank_pool.tile(
                [P, FEAT], F32, name="out_psum", tag="bank%d" % (AGG_BANKS + j % OUT_BANKS)
            )
            nc.tensor.matmul_mx(
                out=out_psum[:],
                lhsT=agg_codes[j].bitcast(FP8X4),
                lhsT_scale=agg_scales[j],
                rhs=w_codes[:].bitcast(FP8X4),
                rhs_scale=w_scales[:],
                start=True,
                stop=True,
            )
            half = FEAT // 2
            for h in range(2):
                columns = slice(h * half, (h + 1) * half)
                part = result_pool.tile([P, half], F32, name="part%d" % h, bufs=1)
                nc.vector.tensor_tensor(
                    out=part[:], in0=out_psum[:, columns], in1=bias[:, columns], op=mybir.AluOpType.add
                )
                if h == 0:
                    nc.scalar.activation(
                        out=part[:], in_=part[:], func=mybir.ActivationFunctionType.Relu
                    )
                else:
                    nc.vector.tensor_scalar_max(out=part[:], in0=part[:], scalar1=0.0)
                nc.sync.dma_start(out=out[j * P : (j + 1) * P, columns], in_=part[:])

        warm = bank_pool.tile([P, FEAT], F32, name="warm", tag="bank3")
        zeros = keep.tile([P, FEAT], BF16)
        nc.gpsimd.memset(zeros[:], 0.0)
        for i in range(0):
            nc.tensor.matmul(out=warm[:], lhsT=zeros[:, :P], rhs=zeros[:], start=True, stop=True)
        head_transpose(0)
        for i in range(0):
            nc.tensor.matmul(out=warm[:], lhsT=zeros[:, :P], rhs=zeros[:], start=True, stop=True)
        f_grouped = regroup_features(0)
        head_transpose(1)
        for i in range(2):
            nc.tensor.matmul(out=warm[:], lhsT=zeros[:, :P], rhs=zeros[:], start=True, stop=True)
        for g in range(A_PASSES):
            head_quantise(g)
            quantise(f_grouped[:], f_codes[:, g, :], f_scales[:, g, :])
            if g + 1 < A_PASSES:
                f_grouped = regroup_features(g + 1)
            if g + 2 < A_PASSES:
                head_transpose(g + 2)
            if g == A_PASSES - 2:
                transpose_a(0, 0)
            if g == A_PASSES - 1:
                transpose_a(0, 1)
            head_multiply(g)
        for j in tiles_of(1):
            order_words(j)
        w_grouped = regroup_weights()
        quantise_a(0)
        agg_rounded = keep.tile([P, FEAT_BLOCKS, HEAD_NODES], BF16)
        for t in range(FEAT_BLOCKS):
            if t < FEAT_BLOCKS - 0:
                nc.scalar.copy(out=agg_rounded[:, t, :], in_=head_agg[t][:])
            else:
                nc.vector.tensor_copy(out=agg_rounded[:, t, :], in_=head_agg[t][:])
        quantise(w_grouped[:], w_codes[:], w_scales[:])
        transpose_a(1, 0)
        transpose_a(1, 1)

        def spread_bias():
            bias_psum = bank_pool.tile([P, FEAT], F32, name="bias_psum", tag="bank2")
            nc.tensor.matmul(out=bias_psum[:], lhsT=ones[:], rhs=bias_row[:], start=True, stop=True)
            nc.vector.tensor_copy(out=bias[:], in_=bias_psum[:])

        def head_codes_of(h):
            grouped = stream.tile([P, ROUND_NODES, PACK], BF16, name="agg_grouped", align_bytes=64)
            nodes = slice(h * ROUND_NODES, (h + 1) * ROUND_NODES)
            nc.vector.tensor_copy(
                out=grouped[:], in_=agg_rounded[:, :, nodes].rearrange("p t n -> p n t")
            )
            quantise_agg(
                grouped[:].rearrange("p n t -> p (n t)"), ROUND_NODES, h * TILES_PER_ROUND
            )

        waiting = list(range(HEAD_TILES))
        ordered_ahead = [11, 13, 15]
        counts = [0, 3, 3, 3, 3, 2]
        for i in range(ROUNDS):
            if i < 2:
                head_codes_of(i)
            if i + 1 < ROUNDS:
                quantise_a(i + 1)
            now = waiting[: counts[i]]
            waiting = waiting[counts[i] :] + list(tiles_of(i))
            alternate = True

            def between():
                if i + 2 < ROUNDS and alternate:
                    transpose_a(i + 2, 0)
                if i == 0:
                    spread_bias()
                for j in now[:2]:
                    project(j)
                for j in now[:2]:
                    if False:
                        relu_on_vector(j)
                if i + 3 < ROUNDS:
                    for j in tiles_of(i + 3):
                        if j in ordered_ahead:
                            order_words(j)

            if i < ROUNDS - 2:
                aggregate(i, between)
            else:
                aggregate_tiles(i, between)
            for j in now[2:]:
                project(j)
                relu_on_vector(j)
            if i + 2 < ROUNDS:
                if not alternate:
                    transpose_a(i + 2, 0)
                transpose_a(i + 2, 1)
            for j in now[:2]:
                if not (False):
                    relu_on_scalar(j)
        for j in waiting[:-1]:
            project(j)
            relu_on_vector(j)
        project_last(waiting[-1])
